import numpy as np
import ml_dtypes


def mxq(x, axis, fmt="e4m3"):
    dtype, down = {"e4m3": (ml_dtypes.float8_e4m3fn, 7), "e5m2": (ml_dtypes.float8_e5m2, 14)}[fmt]
    v = np.moveaxis(np.asarray(x, np.float32).astype(ml_dtypes.bfloat16).astype(np.float64), axis, -1)
    blocks = v.reshape(v.shape[:-1] + (-1, 32))
    amax = np.abs(blocks).max(-1, keepdims=True)
    byte = np.maximum(np.where(amax > 0, np.frexp(amax)[1] - 1 + 127, 0) - down, 1)
    scale = np.exp2(byte - 127.0)
    codes = (blocks / scale).astype(np.float32).astype(dtype).astype(np.float64)
    return np.moveaxis((codes * scale).reshape(v.shape), -1, axis)


WIDE = False


def mx_kscale(k):
    if not WIDE:
        return np.ones(k)
    levels = np.array([10, -10, 5, -5, 0])
    a = np.random.permutation(np.resize(levels, k // 512 * 4)).reshape(k // 512, 4)
    idx = np.arange(k)
    return np.exp2(a[idx // 512, idx % 128 // 32])


BF16 = ml_dtypes.bfloat16


def bf(x):
    return np.asarray(x, np.float32).astype(BF16)


def f64(x):
    return np.asarray(x).astype(np.float64)


B, L, C = 128, 64, 512
LEVELS = 3
ISQ2 = 0.7071067811865476
LC = L // 2 ** LEVELS


def dwt_haar(a):
    e, o = a[:, 0::2], a[:, 1::2]
    return (e + o) * ISQ2, (e - o) * ISQ2


def idwt_haar(a, d):
    nb, n, c = a.shape
    e = (a + d) * ISQ2
    o = (a - d) * ISQ2
    return np.stack([e, o], axis=2).reshape(nb, 2 * n, c)


def gelu_tanh(v):
    return 0.5 * v * (1.0 + np.tanh(np.sqrt(2.0 / np.pi) * (v + 0.044715 * v**3)))


def mix(a, w):
    return (mxq(a, 2, "e4m3").transpose(1, 0, 2) @ mxq(w, 0, "e4m3").transpose(2, 0, 1)).transpose(1, 0, 2)


def setup_inputs():
    s = mx_kscale(C)
    p = np.minimum(s, 1.0)
    x = np.random.standard_normal((B, LC, C)) * s
    for j in range(LEVELS):
        x = idwt_haar(x, np.random.standard_normal((B, LC * 2 ** j, C)) * (s if j == 0 else p))
    return {"x": bf(x),
            "w_approx": bf(np.random.standard_normal((C, C, LC)) / np.sqrt(C) / s[:, None, None]),
            "w_detail": bf(np.random.standard_normal((C, C, LC)) / np.sqrt(C) / s[:, None, None]),
            "W_skip": bf(np.random.standard_normal((C, C)) / np.sqrt(C) / s[:, None]),
            "b_skip": bf(np.random.standard_normal(C) * 0.3)}


def wavelet_conv1d(x, w_approx, w_detail):
    a = x
    details = []
    for _ in range(LEVELS):
        a, d = dwt_haar(a)
        details.append(d)
    a = mix(a, w_approx)
    details[-1] = mix(details[-1], w_detail)
    for d in reversed(details):
        a = idwt_haar(a, d)
    return a


def reference(x, w_approx, w_detail, W_skip, b_skip):
    x = f64(x)
    y = wavelet_conv1d(x, f64(w_approx), f64(w_detail))
    shortcut = (mxq(x, 2, "e4m3") @ mxq(f64(W_skip), 0, "e4m3")) + f64(b_skip)
    return gelu_tanh(y + shortcut)

from contextlib import ExitStack

import concourse.bass as bass
import concourse.mybir as mybir
import concourse.tile as tile
from concourse.masks import make_identity

F32 = mybir.dt.float32
BF16 = mybir.dt.bfloat16
U32 = mybir.dt.uint32
U8 = mybir.dt.uint8
FP8X4 = mybir.dt.float8_e4m3fn_x4
ALU = mybir.AluOpType
ACT = mybir.ActivationFunctionType

P = 128
C = 512
UNITS = 8
R = 0.7071067811865476
R3 = R * R * R
FLOPS = 2 * 8192 * 512 * 512 + 2 * 2 * 8 * 128 * 512 * 512
OC = 256


def tile_waveletblock1d_t_kernel(tc, x, w_approx, w_detail, W_skip, b_skip, out):
    nc = tc.nc
    with ExitStack() as ctx:
        const = ctx.enter_context(tc.tile_pool(name="const", bufs=1))
        xpool = ctx.enter_context(tc.tile_pool(name="xpool", bufs=4))
        ppool = ctx.enter_context(tc.tile_pool(name="ppool", bufs=1))
        hpool = ctx.enter_context(tc.tile_pool(name="hpool", bufs=2))
        gpool = ctx.enter_context(tc.tile_pool(name="gpool", bufs=2))
        apool = ctx.enter_context(tc.tile_pool(name="apool", bufs=2))
        keep = ctx.enter_context(tc.tile_pool(name="keep", bufs=3))
        psum = ctx.enter_context(tc.psum_pool(name="psum", bufs=2))

        ident = const.tile([P, P], F32)
        make_identity(nc, ident[:])
        bias_b = const.tile([P, C], BF16)
        nc.sync.dma_start(out=bias_b[:], in_=b_skip.partition_broadcast(P))
        bias4 = const.tile([P, C], F32)
        nc.vector.tensor_scalar(out=bias4[:], in0=bias_b[:], scalar1=4.0, scalar2=None, op0=ALU.mult)

        ws_codes = const.tile([P, C], U32, align_bytes=64)
        ws_scales = const.tile([P, C], U8, align_bytes=64)
        w_codes = []
        w_scales = []
        for s in range(2):
            wc = const.tile([P, UNITS * C], U32, align_bytes=64, name="wc%d" % s)
            wsc = const.tile([P, UNITS * C], U8, align_bytes=64, name="wsc%d" % s)
            w_codes.append(wc)
            w_scales.append(wsc)

        xus = {}

        def load_x(u):
            xu = xpool.tile([P, 8 * C], BF16, tag="xu", name="xu%d" % u)
            nc.sync.dma_start(out=xu[:], in_=x[:, 8 * u : 8 * u + 8, :].rearrange("b l c -> b (l c)"))
            xus[u] = xu

        state = {}

        def stage_a(u):
            xu = xus[u]
            xv = xu[:].rearrange("p (k two c) -> p k two c", two=2, c=C)
            pp = ppool.tile([P, 4 * C], F32, tag="pp", name="pp%d" % u)
            nc.gpsimd.tensor_tensor(
                out=pp[:].rearrange("p (k c) -> p k c", c=C), in0=xv[:, :, 0, :], in1=xv[:, :, 1, :], op=ALU.add
            )
            pv = pp[:].rearrange("p (h two c) -> p h two c", two=2, c=C)
            s4 = hpool.tile([P, 2 * C], F32, tag="s4", name="s4_%d" % u)
            nc.gpsimd.tensor_tensor(
                out=s4[:].rearrange("p (h c) -> p h c", c=C), in0=pv[:, :, 0, :], in1=pv[:, :, 1, :], op=ALU.add
            )
            ad = hpool.tile([P, 2 * C], F32, tag="ad", name="ad%d" % u)
            nc.gpsimd.tensor_tensor(out=ad[:, 0:C], in0=s4[:, 0:C], in1=s4[:, C : 2 * C], op=ALU.add)
            nc.gpsimd.tensor_tensor(out=ad[:, C : 2 * C], in0=s4[:, 0:C], in1=s4[:, C : 2 * C], op=ALU.subtract)
            mm = keep.tile([P, 2 * C], F32, tag="mm", name="mm%d" % u)
            nc.gpsimd.tensor_tensor(
                out=mm[:].rearrange("p (h c) -> p h c", c=C),
                in0=s4[:].rearrange("p (h c) -> p h c", c=C),
                in1=bias4[:].unsqueeze(1).to_broadcast([P, 2, C]),
                op=ALU.subtract,
            )
            xw = xu[:].bitcast(F32)
            xg = gpool.tile([P, 8 * C], BF16, align_bytes=64, tag="xg", name="xg%d" % u)
            xgw = xg[:].bitcast(F32)
            for jp in range(4):
                tin = psum.tile([P, C], F32, tag="tin", name="tin%d_%d" % (u, jp))
                for jj in range(2):
                    j = 2 * jp + jj
                    for uu in range(2):
                        nc.tensor.transpose(
                            tin[:, uu * 256 + jj * P : uu * 256 + jj * P + P],
                            xw[:, j * 256 + uu * P : j * 256 + uu * P + P],
                            ident[:],
                        )
                nc.scalar.copy(
                    out=xgw[:, jp * C : (jp + 1) * C].rearrange("p (n u) -> p n u", u=2),
                    in_=tin[:].rearrange("p (u n) -> p n u", u=2),
                )
            x_codes = keep.tile([P, 8 * P], U32, align_bytes=64, tag="xc", name="xc%d" % u)
            x_scales = keep.tile([P, 8 * P], U8, align_bytes=64, tag="xs", name="xs%d" % u)
            nc.vector.quantize_mx(out=x_codes[:].bitcast(FP8X4), scales=x_scales[:], in_=xg[:])
            gq = apool.tile([P, 3 * C], BF16, align_bytes=64, tag="gq", name="gq%d" % u)
            for s in range(2):
                at = psum.tile([P, C], F32, tag="at", name="at%d_%d" % (u, s))
                for t in range(4):
                    nc.tensor.transpose(
                        at[:, t * P : (t + 1) * P], ad[:, s * C + t * P : s * C + (t + 1) * P], ident[:]
                    )
                av = at[:].rearrange("p (t b) -> p b t", t=4)
                nc.scalar.activation(
                    out=gq[:, s * C : (s + 1) * C].rearrange("p (b t) -> p b t", t=4), in_=av, func=ACT.Copy, scale=R3
                )
                if s == 1:
                    nc.scalar.activation(
                        out=gq[:, 2 * C : 3 * C].rearrange("p (b t) -> p b t", t=4), in_=av, func=ACT.Copy, scale=-R3
                    )
            a_codes = keep.tile([P, 3 * P], U32, align_bytes=64, tag="ac", name="ac%d" % u)
            a_scales = keep.tile([P, 3 * P], U8, align_bytes=64, tag="as", name="as%d" % u)
            nc.vector.quantize_mx(
                out=a_codes[:, 0 : 2 * P].bitcast(FP8X4), scales=a_scales[:, 0 : 2 * P], in_=gq[:, 0 : 2 * C]
            )
            nc.vector.quantize_mx(
                out=a_codes[:, 2 * P : 3 * P].bitcast(FP8X4), scales=a_scales[:, 2 * P : 3 * P], in_=gq[:, 2 * C : 3 * C]
            )
            state[u] = (mm, x_codes, x_scales, a_codes, a_scales)

        wsraw = xpool.tile([P, 8 * C], BF16, tag="xu", name="wsraw")
        nc.sync.dma_start(
            out=wsraw[:, 0 : 4 * C].rearrange("p (u r) -> p u r", u=2),
            in_=W_skip.rearrange("(u q e) o -> q u (e o)", u=2, e=2),
        )
        load_x(0)
        with tc.tile_pool(name="wstage", bufs=2) as wstage:
            wsg = wstage.tile([P, 8 * OC * 4], BF16, align_bytes=64, tag="wg", name="wsg")
            nc.vector.tensor_copy(
                out=wsg[:, 0 : 4 * C].rearrange("p (o t) -> p o t", t=4),
                in_=wsraw[:, 0 : 4 * C].rearrange("p (t o) -> p o t", t=4),
            )
            nc.vector.quantize_mx(out=ws_codes[:].bitcast(FP8X4), scales=ws_scales[:], in_=wsg[:, 0 : 4 * C])
            raws = []
            for s, w in enumerate((w_approx, w_detail)):
                wv = w.rearrange("(t p) o l -> p t o l", p=P)
                for ch in range(C // OC):
                    wraw = wstage.tile([P, 4 * OC * 8], BF16, tag="wraw", name="wraw%d_%d" % (s, ch))
                    nc.sync.dma_start(
                        out=wraw[:].rearrange("p (t r) -> p t r", t=4),
                        in_=wv[:, :, ch * OC : (ch + 1) * OC, :].rearrange("p t o l -> p t (o l)"),
                    )
                    raws.append((s, ch, wraw))
                    if ch == 1:
                        load_x(1 + s)
            stage_a(0)
            for s, ch, wraw in raws:
                wg = wstage.tile([P, 8 * OC * 4], BF16, align_bytes=64, tag="wg", name="wg%d_%d" % (s, ch))
                src = wraw[:].rearrange("p (t o l) -> p l o t", t=4, l=8)
                dst = wg[:].rearrange("p (l o t) -> p l o t", l=8, t=4)
                nc.vector.tensor_copy(out=dst[:, 0:4], in_=src[:, 0:4])
                nc.scalar.copy(out=dst[:, 5:8], in_=src[:, 5:8])
                nc.vector.tensor_copy(out=dst[:, 4], in_=src[:, 4])
                for l in range(8):
                    nc.vector.quantize_mx(
                        out=w_codes[s][:, l * C + ch * OC : l * C + (ch + 1) * OC].bitcast(FP8X4),
                        scales=w_scales[s][:, l * C + ch * OC : l * C + (ch + 1) * OC],
                        in_=wg[:, l * OC * 4 : (l + 1) * OC * 4],
                    )
                if ch == 1:
                    stage_a(1 + s)

        zpool = ctx.enter_context(tc.tile_pool(name="zpool", bufs=4))

        def stage_b(u):
            xu = xus[u]
            mm, x_codes, x_scales, a_codes, a_scales = state[u]
            cc = hpool.tile([P, 2 * C], F32, tag="cc", name="cc%d" % u)
            for h in range(2):
                mx = psum.tile([P, C], F32, tag="mix", name="mix%d_%d" % (u, h))
                nc.tensor.matmul_mx(
                    out=mx[:],
                    lhsT=a_codes[:, 0:P].bitcast(FP8X4),
                    lhsT_scale=a_scales[:, 0:P],
                    rhs=w_codes[0][:, u * C : (u + 1) * C].bitcast(FP8X4),
                    rhs_scale=w_scales[0][:, u * C : (u + 1) * C],
                    start=True,
                    stop=False,
                )
                nc.tensor.matmul_mx(
                    out=mx[:],
                    lhsT=a_codes[:, (1 + h) * P : (2 + h) * P].bitcast(FP8X4),
                    lhsT_scale=a_scales[:, (1 + h) * P : (2 + h) * P],
                    rhs=w_codes[1][:, u * C : (u + 1) * C].bitcast(FP8X4),
                    rhs_scale=w_scales[1][:, u * C : (u + 1) * C],
                    start=False,
                    stop=True,
                )
                nc.vector.scalar_tensor_tensor(
                    out=cc[:, h * C : (h + 1) * C],
                    in0=mx[:],
                    scalar=-4.0 * R3,
                    in1=mm[:, h * C : (h + 1) * C],
                    op0=ALU.mult,
                    op1=ALU.add,
                )
                z = zpool.tile([P, 4 * C], F32, tag="z", name="z%d_%d" % (u, h))
                nc.vector.scalar_tensor_tensor(
                    out=z[:].rearrange("p (j c) -> p j c", c=C),
                    in0=cc[:, h * C : (h + 1) * C].unsqueeze(1).to_broadcast([P, 4, C]),
                    scalar=-0.25,
                    in1=xu[:, h * 4 * C : (h + 1) * 4 * C].rearrange("p (j c) -> p j c", c=C),
                    op0=ALU.mult,
                    op1=ALU.add,
                )
                for jj in range(4):
                    j = 4 * h + jj
                    sk = psum.tile([P, C], F32, tag="sk", name="sk%d_%d" % (u, j))
                    nc.tensor.matmul_mx(
                        out=sk[:],
                        lhsT=x_codes[:, j * P : (j + 1) * P].bitcast(FP8X4),
                        lhsT_scale=x_scales[:, j * P : (j + 1) * P],
                        rhs=ws_codes[:].bitcast(FP8X4),
                        rhs_scale=ws_scales[:],
                        start=True,
                        stop=True,
                    )
                    nc.vector.tensor_tensor(
                        out=z[:, jj * C : (jj + 1) * C], in0=sk[:], in1=z[:, jj * C : (jj + 1) * C], op=ALU.add
                    )
                nc.scalar.activation(out=z[:], in_=z[:], func=ACT.Gelu_apprx_tanh)
                nc.scalar.dma_start(
                    out=out[:, 8 * u + 4 * h : 8 * u + 4 * h + 4, :].rearrange("b l o -> b (l o)"), in_=z[:]
                )

        for u in range(UNITS):
            if u + 3 < UNITS:
                load_x(u + 3)
            stage_b(u)
            if u + 3 < UNITS:
                stage_a(u + 3)
